import numpy as np
import ml_dtypes


def mxq(x, axis, fmt="e4m3"):
    dtype, down = {"e4m3": (ml_dtypes.float8_e4m3fn, 7), "e5m2": (ml_dtypes.float8_e5m2, 14)}[fmt]
    v = np.moveaxis(np.asarray(x, np.float32).astype(ml_dtypes.bfloat16).astype(np.float64), axis, -1)
    blocks = v.reshape(v.shape[:-1] + (-1, 32))
    amax = np.abs(blocks).max(-1, keepdims=True)
    byte = np.maximum(np.where(amax > 0, np.frexp(amax)[1] - 1 + 127, 0) - down, 1)
    scale = np.exp2(byte - 127.0)
    codes = (blocks / scale).astype(np.float32).astype(dtype).astype(np.float64)
    return np.moveaxis((codes * scale).reshape(v.shape), -1, axis)


WIDE = False


def mx_kscale(k):
    if not WIDE:
        return np.ones(k)
    levels = np.array([10, -10, 5, -5, 0])
    if k % 512:
        return np.exp2(np.random.permutation(np.resize(levels, k // 32))).repeat(32)
    a = np.empty((k // 512, 16))
    for p in range(k // 512):
        a[p, :8] = np.random.permutation(np.resize(levels, 8))
        for g in range(8):
            far = levels[np.abs(levels - a[p, g]) >= 10]
            a[p, g + 8] = far[np.random.randint(len(far))]
    return np.exp2(a.ravel()).repeat(32)


BF16 = ml_dtypes.bfloat16


def bf(x):
    return np.asarray(x, np.float32).astype(BF16)


def f64(x):
    return np.asarray(x).astype(np.float64)


B, NW, N, D, J = 4, 4, 512, 128, 3
KEEP = (0.0625, 0.0625, 0.25, 1.0)


def draw_power(j, a):
    r = np.random.uniform(size=(B, NW, N, N)) * (np.random.uniform(size=(B, NW, N, N)) < KEEP[j])
    t = r / r.sum(-1, keepdims=True)
    c = 0.5 ** (2 ** j)
    p = c * np.eye(N) + (1.0 - c) * t
    return bf(p * a[:, None] / a[None, :])


def setup_inputs():
    s = mx_kscale(N)
    a = s / s.max()
    alpha = np.random.uniform(size=(NW, D))
    x = np.random.standard_normal((B, NW, N, D)) * alpha[None, :, None, :] * a[:, None]
    return {"x_nodes": bf(x), "p1": draw_power(0, a), "p2": draw_power(1, a), "p4": draw_power(2, a), "p8": draw_power(3, a)}


def reference(x_nodes, p1, p2, p4, p8):
    X = f64(x_nodes)
    powers = [f64(p1), f64(p2), f64(p4), f64(p8)]
    psi = [mxq(powers[j] - powers[j + 1], 3, "e4m3") for j in range(J)]
    Xq = mxq(X, 2, "e4m3")
    first = [np.abs(psi[j] @ Xq) for j in range(J)]
    firstq = [mxq(first[j], 2, "e4m3") for j in range(J - 1)]
    second = [np.abs(psi[k] @ firstq[j]) for j in range(J) for k in range(j + 1, J)]
    feats = np.concatenate([X] + first + second, axis=-1)
    pooled = feats.mean(axis=2)
    return pooled.reshape(B, -1)

@@ -1,0 +1,225 @@
+from contextlib import ExitStack
+
+import concourse.mybir as mybir
+from concourse.masks import make_identity
+
+F32 = mybir.dt.float32
+BF16 = mybir.dt.bfloat16
+U32 = mybir.dt.uint32
+U8 = mybir.dt.uint8
+FP8X4 = mybir.dt.float8_e4m3fn_x4
+ABS = mybir.ActivationFunctionType.Abs
+COPY = mybir.ActivationFunctionType.Copy
+
+CLOUDS = 4
+WEIGHTINGS = 4
+SETS = CLOUDS * WEIGHTINGS
+POINTS = 512
+FEATS = 128
+P = 128
+SLOTS = 4
+HALVES = 2
+WAVELETS = 3
+BLOCKS = 7
+BANK = 512
+ROW_TILES_PER_BANK = BANK // (HALVES * P)
+ONES_COLS = 32
+LOADS_AHEAD = 3
+
+FLOPS = 2 * POINTS * POINTS * FEATS * 6 * SETS
+
+
+def tile_simplicialfeatlearninglayertri_pb_t_kernel(tc, x_nodes, p1, p2, p4, p8, out):
+    nc = tc.nc
+    operators = (p1, p2, p4, p8)
+
+    with ExitStack() as ctx:
+        const = ctx.enter_context(tc.tile_pool(name="const", bufs=1))
+        load = ctx.enter_context(tc.tile_pool(name="load", bufs=LOADS_AHEAD))
+        work = ctx.enter_context(tc.tile_pool(name="work", bufs=2))
+        pair_psum = ctx.enter_context(tc.psum_pool(name="pair_psum", bufs=4))
+        mx_psum = ctx.enter_context(tc.psum_pool(name="mx_psum", bufs=4))
+
+        identity = const.tile([P, P], F32)
+        make_identity(nc, identity[:])
+        ones = const.tile([P, ONES_COLS], BF16)
+        nc.vector.memset(ones[:], 1.0)
+        sums = const.tile([P, P], F32)
+        nc.vector.memset(sums[:], 0.0)
+        sums_by_set = sums[:, 0 : SETS * BLOCKS].rearrange("d (s i) -> d s i", i=BLOCKS)
+
+        x_rows, x_mx = {}, {}
+        power_rows, psi_rows, psi_grouped, psi_mx, f_grouped, f_mx = {}, {}, {}, {}, {}, {}
+
+        def load_cloud(b):
+            rows = work.tile([P, WEIGHTINGS * SLOTS * FEATS], BF16, tag="x_rows")
+            nc.sync.dma_start(
+                out=rows[:].rearrange("c (w r) -> c w r", w=WEIGHTINGS),
+                in_=x_nodes[b].rearrange("w (c t) d -> c w (t d)", t=SLOTS),
+            )
+            x_rows[b] = rows
+
+        def prepare_cloud(b):
+            rows = x_rows[b]
+            grouped = work.tile([P, WEIGHTINGS * FEATS * SLOTS], BF16, tag="x_grouped", align_bytes=64)
+            nc.vector.tensor_copy(
+                out=grouped[:].rearrange("c (w d t) -> c w d t", w=WEIGHTINGS, t=SLOTS),
+                in_=rows[:].rearrange("c (w t d) -> c w d t", w=WEIGHTINGS, t=SLOTS),
+            )
+            codes = work.tile([P, WEIGHTINGS * FEATS], U32, tag="x_codes", align_bytes=64)
+            scales = work.tile([P, WEIGHTINGS * FEATS], U8, tag="x_scales", align_bytes=64)
+            nc.vector.quantize_mx(out=codes[:].bitcast(FP8X4), scales=scales[:], in_=grouped[:])
+            x_mx[b] = (codes, scales)
+
+            bank = mx_psum.tile([P, BANK], F32, tag="mx")
+            for w in range(WEIGHTINGS):
+                for t in range(SLOTS):
+                    first = (w * SLOTS + t) * FEATS
+                    nc.tensor.matmul(
+                        out=bank[:, w * ONES_COLS : (w + 1) * ONES_COLS],
+                        lhsT=rows[:, first : first + FEATS],
+                        rhs=ones[:],
+                        start=(t == 0),
+                        stop=(t == SLOTS - 1),
+                    )
+            nc.scalar.copy(
+                out=sums_by_set[:, b * WEIGHTINGS : (b + 1) * WEIGHTINGS, 0],
+                in_=bank[:, 0 : WEIGHTINGS * ONES_COLS].rearrange("d (w r) -> d w r", r=ONES_COLS)[:, :, 0],
+            )
+
+        def load_set(s):
+            b, w = divmod(s, WEIGHTINGS)
+            power_rows[s] = []
+            for j, operator in enumerate(operators):
+                rows = load.tile([P, SLOTS * POINTS], BF16, tag="power%d" % j)
+                nc.sync.dma_start(
+                    out=rows[:],
+                    in_=operator[b, w].rearrange("(q t) m -> q (t m)", t=SLOTS),
+                )
+                power_rows[s].append(rows)
+
+        def subtract(s):
+            psi_rows[s] = []
+            for j in range(WAVELETS):
+                rows = work.tile([P, SLOTS * POINTS], BF16, tag="psi%d" % j)
+                nc.vector.tensor_sub(out=rows[:], in0=power_rows[s][j][:], in1=power_rows[s][j + 1][:])
+                psi_rows[s].append(rows)
+
+        def transpose(s):
+            psi_grouped[s] = []
+            for j in range(WAVELETS):
+                pairs = psi_rows[s][j][:].bitcast(F32)
+                grouped = work.tile([P, POINTS * SLOTS], BF16, tag="grouped%d" % j, align_bytes=64)
+                grouped_pairs = grouped[:].bitcast(F32)
+                for h in range(SLOTS // ROW_TILES_PER_BANK):
+                    bank = pair_psum.tile([P, BANK], F32, tag="pairs")
+                    for i in range(BANK // P):
+                        first = h * BANK + (i // HALVES) * HALVES * P + i % HALVES
+                        nc.tensor.transpose(
+                            out=bank[:, i * P : (i + 1) * P],
+                            in_=pairs[:, first : first + HALVES * P - i % HALVES : HALVES],
+                            identity=identity[:],
+                        )
+                    copy = nc.vector.tensor_copy if (j * 2 + h) % 3 == 1 else nc.scalar.copy
+                    copy(
+                        out=grouped_pairs[:, h * BANK : (h + 1) * BANK].rearrange(
+                            "c (a q u) -> c a q u", a=ROW_TILES_PER_BANK, u=HALVES
+                        ),
+                        in_=bank[:].rearrange("c (a u q) -> c a q u", a=ROW_TILES_PER_BANK, u=HALVES),
+                    )
+                psi_grouped[s].append(grouped)
+
+        def quantise_psi(s):
+            psi_mx[s] = []
+            for j in range(WAVELETS):
+                codes = work.tile([P, POINTS], U32, tag="psi_codes%d" % j, align_bytes=64)
+                scales = work.tile([P, POINTS], U8, tag="psi_scales%d" % j, align_bytes=64)
+                nc.vector.quantize_mx(
+                    out=codes[:].bitcast(FP8X4), scales=scales[:], in_=psi_grouped[s][j][:]
+                )
+                psi_mx[s].append((codes, scales))
+
+        def mx_pass(acc, stationary, stationary_cols, moving, moving_cols):
+            nc.tensor.matmul_mx(
+                out=acc,
+                lhsT=stationary[0][:, stationary_cols].bitcast(FP8X4),
+                lhsT_scale=stationary[1][:, stationary_cols],
+                rhs=moving[0][:, moving_cols].bitcast(FP8X4),
+                rhs_scale=moving[1][:, moving_cols],
+                start=True,
+                stop=True,
+            )
+
+        def pool_product(s, block, features, feature_cols, psi):
+            bank = mx_psum.tile([P, BANK], F32, tag="mx")
+            mx_pass(bank[:], features, feature_cols, psi, slice(0, POINTS))
+            absolute = work.tile([P, BANK], BF16, tag="absolute")
+            nc.scalar.activation(
+                out=absolute[:], in_=bank[:], func=ABS, accum_out=sums_by_set[:, s, block : block + 1]
+            )
+
+        def first_layer(s):
+            b, w = divmod(s, WEIGHTINGS)
+            x_cols = slice(w * FEATS, (w + 1) * FEATS)
+            grouped = work.tile([P, 2 * FEATS * SLOTS], BF16, tag="f_grouped", align_bytes=64)
+            for j in range(2):
+                bank = mx_psum.tile([P, BANK], F32, tag="mx")
+                for t in range(SLOTS):
+                    cols = slice(t * P, (t + 1) * P)
+                    mx_pass(bank[:, cols], psi_mx[s][j], cols, x_mx[b], x_cols)
+                nc.scalar.activation(
+                    out=grouped[:, j * BANK : (j + 1) * BANK].rearrange("c (d t) -> c d t", t=SLOTS),
+                    in_=bank[:].rearrange("c (t d) -> c d t", t=SLOTS),
+                    func=ABS,
+                )
+            f_grouped[s] = grouped
+            for j in range(WAVELETS):
+                pool_product(s, 1 + j, x_mx[b], x_cols, psi_mx[s][j])
+
+        def quantise_f(s):
+            codes = work.tile([P, 2 * FEATS], U32, tag="f_codes", align_bytes=64)
+            scales = work.tile([P, 2 * FEATS], U8, tag="f_scales", align_bytes=64)
+            nc.vector.quantize_mx(out=codes[:].bitcast(FP8X4), scales=scales[:], in_=f_grouped[s][:])
+            f_mx[s] = (codes, scales)
+
+        def second_layer(s):
+            block = 1 + WAVELETS
+            for j in range(WAVELETS):
+                for k in range(j + 1, WAVELETS):
+                    pool_product(s, block, f_mx[s], slice(j * FEATS, (j + 1) * FEATS), psi_mx[s][k])
+                    block += 1
+
+        def load_ahead(s):
+            if s < SETS:
+                if s % WEIGHTINGS == 0:
+                    load_cloud(s // WEIGHTINGS)
+                load_set(s)
+
+        for s in range(LOADS_AHEAD):
+            load_ahead(s)
+        prepare_cloud(0)
+        subtract(0)
+        transpose(0)
+        quantise_psi(0)
+        for s in range(SETS):
+            following = s + 1
+            load_ahead(s + LOADS_AHEAD)
+            if following < SETS:
+                subtract(following)
+            first_layer(s)
+            if following < SETS:
+                transpose(following)
+            quantise_f(s)
+            if following < SETS:
+                quantise_psi(following)
+            if s % WEIGHTINGS == WEIGHTINGS - 2 and s + 2 < SETS:
+                prepare_cloud((s + 2) // WEIGHTINGS)
+            second_layer(s)
+
+        bank = mx_psum.tile([P, BANK], F32, tag="mx")
+        nc.tensor.transpose(out=bank[:, 0:P], in_=sums[:], identity=identity[:])
+        means = const.tile([P, FEATS], F32)
+        nc.scalar.activation(out=means[:], in_=bank[:, 0:P], func=COPY, scale=1.0 / POINTS)
+        nc.sync.dma_start(
+            out=out.rearrange("b (r d) -> (b r) d", d=FEATS), in_=means[0 : SETS * BLOCKS, :]
+        )

@@ -49,7 +49,8 @@ def tile_simplicialfeatlearninglayertri_pb_t_kernel(tc, x_nodes, p1, p2, p4, p8,
         sums_by_set = sums[:, 0 : SETS * BLOCKS].rearrange("d (s i) -> d s i", i=BLOCKS)
 
         x_rows, x_mx = {}, {}
-        power_rows, psi_rows, psi_grouped, psi_mx, f_grouped, f_mx = {}, {}, {}, {}, {}, {}
+        power_rows, psi_rows, psi_grouped, psi_mx = {}, {}, {}, {}
+        f_rows, f_grouped, f_mx = {}, {}, {}
 
         def load_cloud(b):
             rows = work.tile([P, WEIGHTINGS * SLOTS * FEATS], BF16, tag="x_rows")
@@ -120,20 +121,20 @@ def tile_simplicialfeatlearninglayertri_pb_t_kernel(tc, x_nodes, p1, p2, p4, p8,
                             in_=pairs[:, first : first + HALVES * P - i % HALVES : HALVES],
                             identity=identity[:],
                         )
-                    copy = nc.vector.tensor_copy if (j * 2 + h) % 3 == 1 else nc.scalar.copy
+                    copy = nc.vector.tensor_copy if (s * 6 + j * 2 + h) % 5 == 2 else nc.scalar.copy
                     copy(
                         out=grouped_pairs[:, h * BANK : (h + 1) * BANK].rearrange(
-                            "c (a q u) -> c a q u", a=ROW_TILES_PER_BANK, u=HALVES
+                            "c (q a u) -> c q a u", a=ROW_TILES_PER_BANK, u=HALVES
                         ),
-                        in_=bank[:].rearrange("c (a u q) -> c a q u", a=ROW_TILES_PER_BANK, u=HALVES),
+                        in_=bank[:].rearrange("c (a u q) -> c q a u", a=ROW_TILES_PER_BANK, u=HALVES),
                     )
                 psi_grouped[s].append(grouped)
 
         def quantise_psi(s):
             psi_mx[s] = []
             for j in range(WAVELETS):
-                codes = work.tile([P, POINTS], U32, tag="psi_codes%d" % j, align_bytes=64)
-                scales = work.tile([P, POINTS], U8, tag="psi_scales%d" % j, align_bytes=64)
+                codes = work.tile([P, POINTS], U32, tag="psi_codes%d" % j, bufs=3, align_bytes=64)
+                scales = work.tile([P, POINTS], U8, tag="psi_scales%d" % j, bufs=3, align_bytes=64)
                 nc.vector.quantize_mx(
                     out=codes[:].bitcast(FP8X4), scales=scales[:], in_=psi_grouped[s][j][:]
                 )
@@ -150,31 +151,44 @@ def tile_simplicialfeatlearninglayertri_pb_t_kernel(tc, x_nodes, p1, p2, p4, p8,
                 stop=True,
             )
 
-        def pool_product(s, block, features, feature_cols, psi):
+        def pool_product(s, block, features, feature_cols, psi, absolute):
             bank = mx_psum.tile([P, BANK], F32, tag="mx")
             mx_pass(bank[:], features, feature_cols, psi, slice(0, POINTS))
-            absolute = work.tile([P, BANK], BF16, tag="absolute")
             nc.scalar.activation(
-                out=absolute[:], in_=bank[:], func=ABS, accum_out=sums_by_set[:, s, block : block + 1]
+                out=absolute, in_=bank[:], func=ABS, accum_out=sums_by_set[:, s, block : block + 1]
             )
 
         def first_layer(s):
             b, w = divmod(s, WEIGHTINGS)
             x_cols = slice(w * FEATS, (w + 1) * FEATS)
-            grouped = work.tile([P, 2 * FEATS * SLOTS], BF16, tag="f_grouped", align_bytes=64)
-            for j in range(2):
-                bank = mx_psum.tile([P, BANK], F32, tag="mx")
-                for t in range(SLOTS):
-                    cols = slice(t * P, (t + 1) * P)
-                    mx_pass(bank[:, cols], psi_mx[s][j], cols, x_mx[b], x_cols)
-                nc.scalar.activation(
-                    out=grouped[:, j * BANK : (j + 1) * BANK].rearrange("c (d t) -> c d t", t=SLOTS),
-                    in_=bank[:].rearrange("c (t d) -> c d t", t=SLOTS),
-                    func=ABS,
-                )
-            f_grouped[s] = grouped
+            rows = work.tile([P, 2 * POINTS], BF16, tag="f_rows", align_bytes=64)
+            f_rows[s] = rows
             for j in range(WAVELETS):
-                pool_product(s, 1 + j, x_mx[b], x_cols, psi_mx[s][j])
+                if j < 2:
+                    absolute = rows[:, j * POINTS : (j + 1) * POINTS]
+                else:
+                    absolute = unread(s)
+                pool_product(s, 1 + j, x_mx[b], x_cols, psi_mx[s][j], absolute)
+
+        def unread(s):
+            tile = work.tile([P, POINTS], BF16, tag="absolute")
+            return tile[:]
+
+        def transpose_f(s):
+            pairs = f_rows[s][:].bitcast(F32)
+            bank = pair_psum.tile([P, BANK], F32, tag="pairs")
+            for i in range(BANK // P):
+                nc.tensor.transpose(
+                    out=bank[:, i * P : (i + 1) * P],
+                    in_=pairs[:, i * P : (i + 1) * P],
+                    identity=identity[:],
+                )
+            grouped = work.tile([P, 2 * FEATS * SLOTS], BF16, tag="f_grouped", align_bytes=64)
+            nc.scalar.copy(
+                out=grouped[:].bitcast(F32).rearrange("c (j d u) -> c j d u", j=2, u=HALVES),
+                in_=bank[:].rearrange("c (j u d) -> c j d u", j=2, u=HALVES),
+            )
+            f_grouped[s] = grouped
 
         def quantise_f(s):
             codes = work.tile([P, 2 * FEATS], U32, tag="f_codes", align_bytes=64)
@@ -186,7 +200,7 @@ def tile_simplicialfeatlearninglayertri_pb_t_kernel(tc, x_nodes, p1, p2, p4, p8,
             block = 1 + WAVELETS
             for j in range(WAVELETS):
                 for k in range(j + 1, WAVELETS):
-                    pool_product(s, block, f_mx[s], slice(j * FEATS, (j + 1) * FEATS), psi_mx[s][k])
+                    pool_product(s, block, f_mx[s], slice(j * FEATS, (j + 1) * FEATS), psi_mx[s][k], unread(s))
                     block += 1
 
         def load_ahead(s):
@@ -209,6 +223,7 @@ def tile_simplicialfeatlearninglayertri_pb_t_kernel(tc, x_nodes, p1, p2, p4, p8,
             first_layer(s)
             if following < SETS:
                 transpose(following)
+            transpose_f(s)
             quantise_f(s)
             if following < SETS:
                 quantise_psi(following)

@@ -24,7 +24,9 @@ BLOCKS = 7
 BANK = 512
 ROW_TILES_PER_BANK = BANK // (HALVES * P)
 ONES_COLS = 32
-LOADS_AHEAD = 3
+LOAD_BUFS = 4
+UNITS = SETS * WAVELETS
+SECOND = ((0, 1), (0, 2), (1, 2))
 
 FLOPS = 2 * POINTS * POINTS * FEATS * 6 * SETS
 
@@ -35,8 +37,8 @@ def tile_simplicialfeatlearninglayertri_pb_t_kernel(tc, x_nodes, p1, p2, p4, p8,
 
     with ExitStack() as ctx:
         const = ctx.enter_context(tc.tile_pool(name="const", bufs=1))
-        load = ctx.enter_context(tc.tile_pool(name="load", bufs=LOADS_AHEAD))
-        work = ctx.enter_context(tc.tile_pool(name="work", bufs=2))
+        load = ctx.enter_context(tc.tile_pool(name="load", bufs=LOAD_BUFS))
+        work = ctx.enter_context(tc.tile_pool(name="work", bufs=3))
         pair_psum = ctx.enter_context(tc.psum_pool(name="pair_psum", bufs=4))
         mx_psum = ctx.enter_context(tc.psum_pool(name="mx_psum", bufs=4))
 
@@ -48,9 +50,8 @@ def tile_simplicialfeatlearninglayertri_pb_t_kernel(tc, x_nodes, p1, p2, p4, p8,
         nc.vector.memset(sums[:], 0.0)
         sums_by_set = sums[:, 0 : SETS * BLOCKS].rearrange("d (s i) -> d s i", i=BLOCKS)
 
-        x_rows, x_mx = {}, {}
-        power_rows, psi_rows, psi_grouped, psi_mx = {}, {}, {}, {}
-        f_rows, f_grouped, f_mx = {}, {}, {}
+        x_rows, x_mx, power_rows, psi_rows, psi_grouped, psi_mx = {}, {}, {}, {}, {}, {}
+        f_rows, f_grouped, f_mx, products = {}, {}, {}, []
 
         def load_cloud(b):
             rows = work.tile([P, WEIGHTINGS * SLOTS * FEATS], BF16, tag="x_rows")
@@ -60,25 +61,39 @@ def tile_simplicialfeatlearninglayertri_pb_t_kernel(tc, x_nodes, p1, p2, p4, p8,
             )
             x_rows[b] = rows
 
-        def prepare_cloud(b):
-            rows = x_rows[b]
-            grouped = work.tile([P, WEIGHTINGS * FEATS * SLOTS], BF16, tag="x_grouped", align_bytes=64)
-            nc.vector.tensor_copy(
-                out=grouped[:].rearrange("c (w d t) -> c w d t", w=WEIGHTINGS, t=SLOTS),
-                in_=rows[:].rearrange("c (w t d) -> c w d t", w=WEIGHTINGS, t=SLOTS),
+        def load_power(s, j):
+            b, w = divmod(s, WEIGHTINGS)
+            rows = load.tile([P, SLOTS * POINTS], BF16, tag="power%d" % j)
+            nc.sync.dma_start(
+                out=rows[:], in_=operators[j][b, w].rearrange("(q t) m -> q (t m)", t=SLOTS)
             )
-            codes = work.tile([P, WEIGHTINGS * FEATS], U32, tag="x_codes", align_bytes=64)
-            scales = work.tile([P, WEIGHTINGS * FEATS], U8, tag="x_scales", align_bytes=64)
-            nc.vector.quantize_mx(out=codes[:].bitcast(FP8X4), scales=scales[:], in_=grouped[:])
-            x_mx[b] = (codes, scales)
+            power_rows[s, j] = rows
 
+        def prepare_x(s):
+            b, w = divmod(s, WEIGHTINGS)
+            grouped = work.tile([P, FEATS * SLOTS], BF16, tag="x_grouped", align_bytes=64)
+            nc.vector.tensor_copy(
+                out=grouped[:].rearrange("c (d t) -> c d t", t=SLOTS),
+                in_=x_rows[b][:, w * SLOTS * FEATS : (w + 1) * SLOTS * FEATS].rearrange(
+                    "c (t d) -> c d t", t=SLOTS
+                ),
+            )
+            x_grouped[s] = grouped
+
+        def quantise_x(s):
+            codes = work.tile([P, FEATS], U32, tag="x_codes", align_bytes=64)
+            scales = work.tile([P, FEATS], U8, tag="x_scales", align_bytes=64)
+            nc.vector.quantize_mx(out=codes[:].bitcast(FP8X4), scales=scales[:], in_=x_grouped[s][:])
+            x_mx[s] = (codes, scales)
+
+        def sum_x(b):
             bank = mx_psum.tile([P, BANK], F32, tag="mx")
             for w in range(WEIGHTINGS):
                 for t in range(SLOTS):
                     first = (w * SLOTS + t) * FEATS
                     nc.tensor.matmul(
                         out=bank[:, w * ONES_COLS : (w + 1) * ONES_COLS],
-                        lhsT=rows[:, first : first + FEATS],
+                        lhsT=x_rows[b][:, first : first + FEATS],
                         rhs=ones[:],
                         start=(t == 0),
                         stop=(t == SLOTS - 1),
@@ -88,91 +103,75 @@ def tile_simplicialfeatlearninglayertri_pb_t_kernel(tc, x_nodes, p1, p2, p4, p8,
                 in_=bank[:, 0 : WEIGHTINGS * ONES_COLS].rearrange("d (w r) -> d w r", r=ONES_COLS)[:, :, 0],
             )
 
-        def load_set(s):
-            b, w = divmod(s, WEIGHTINGS)
-            power_rows[s] = []
-            for j, operator in enumerate(operators):
-                rows = load.tile([P, SLOTS * POINTS], BF16, tag="power%d" % j)
-                nc.sync.dma_start(
-                    out=rows[:],
-                    in_=operator[b, w].rearrange("(q t) m -> q (t m)", t=SLOTS),
-                )
-                power_rows[s].append(rows)
+        def subtract(unit):
+            s, j = divmod(unit, WAVELETS)
+            rows = work.tile([P, SLOTS * POINTS], BF16, tag="psi")
+            nc.vector.tensor_sub(out=rows[:], in0=power_rows[s, j][:], in1=power_rows[s, j + 1][:])
+            psi_rows[unit] = rows
 
-        def subtract(s):
-            psi_rows[s] = []
-            for j in range(WAVELETS):
-                rows = work.tile([P, SLOTS * POINTS], BF16, tag="psi%d" % j)
-                nc.vector.tensor_sub(out=rows[:], in0=power_rows[s][j][:], in1=power_rows[s][j + 1][:])
-                psi_rows[s].append(rows)
-
-        def transpose(s):
-            psi_grouped[s] = []
-            for j in range(WAVELETS):
-                pairs = psi_rows[s][j][:].bitcast(F32)
-                grouped = work.tile([P, POINTS * SLOTS], BF16, tag="grouped%d" % j, align_bytes=64)
-                grouped_pairs = grouped[:].bitcast(F32)
-                for h in range(SLOTS // ROW_TILES_PER_BANK):
-                    bank = pair_psum.tile([P, BANK], F32, tag="pairs")
-                    for i in range(BANK // P):
-                        first = h * BANK + (i // HALVES) * HALVES * P + i % HALVES
-                        nc.tensor.transpose(
-                            out=bank[:, i * P : (i + 1) * P],
-                            in_=pairs[:, first : first + HALVES * P - i % HALVES : HALVES],
-                            identity=identity[:],
-                        )
-                    copy = nc.vector.tensor_copy if (s * 6 + j * 2 + h) % 5 == 2 else nc.scalar.copy
-                    copy(
-                        out=grouped_pairs[:, h * BANK : (h + 1) * BANK].rearrange(
-                            "c (q a u) -> c q a u", a=ROW_TILES_PER_BANK, u=HALVES
-                        ),
-                        in_=bank[:].rearrange("c (a u q) -> c q a u", a=ROW_TILES_PER_BANK, u=HALVES),
+        def transpose(unit):
+            pairs = psi_rows[unit][:].bitcast(F32)
+            grouped = work.tile([P, POINTS * SLOTS], BF16, tag="psi_grouped", align_bytes=64)
+            grouped_pairs = grouped[:].bitcast(F32)
+            for h in range(SLOTS // ROW_TILES_PER_BANK):
+                bank = pair_psum.tile([P, BANK], F32, tag="pairs")
+                for i in range(BANK // P):
+                    first = h * BANK + (i // HALVES) * HALVES * P + i % HALVES
+                    nc.tensor.transpose(
+                        out=bank[:, i * P : (i + 1) * P],
+                        in_=pairs[:, first : first + HALVES * P - i % HALVES : HALVES],
+                        identity=identity[:],
                     )
-                psi_grouped[s].append(grouped)
-
-        def quantise_psi(s):
-            psi_mx[s] = []
-            for j in range(WAVELETS):
-                codes = work.tile([P, POINTS], U32, tag="psi_codes%d" % j, bufs=3, align_bytes=64)
-                scales = work.tile([P, POINTS], U8, tag="psi_scales%d" % j, bufs=3, align_bytes=64)
-                nc.vector.quantize_mx(
-                    out=codes[:].bitcast(FP8X4), scales=scales[:], in_=psi_grouped[s][j][:]
+                copy = nc.vector.tensor_copy if (unit % WAVELETS, h) == (1, 1) else nc.scalar.copy
+                copy(
+                    out=grouped_pairs[:, h * BANK : (h + 1) * BANK].rearrange(
+                        "c (q a u) -> c q a u", a=ROW_TILES_PER_BANK, u=HALVES
+                    ),
+                    in_=bank[:].rearrange("c (a u q) -> c q a u", a=ROW_TILES_PER_BANK, u=HALVES),
                 )
-                psi_mx[s].append((codes, scales))
+            psi_grouped[unit] = grouped
 
-        def mx_pass(acc, stationary, stationary_cols, moving, moving_cols):
+        def quantise_psi(unit):
+            codes = work.tile([P, POINTS], U32, tag="psi_codes%d" % (unit % WAVELETS), align_bytes=64)
+            scales = work.tile([P, POINTS], U8, tag="psi_scales%d" % (unit % WAVELETS), align_bytes=64)
+            nc.vector.quantize_mx(out=codes[:].bitcast(FP8X4), scales=scales[:], in_=psi_grouped[unit][:])
+            psi_mx[unit] = (codes, scales)
+
+        def multiply(s, block, features, feature_cols, psi):
+            bank = mx_psum.tile([P, BANK], F32, tag="mx")
             nc.tensor.matmul_mx(
-                out=acc,
-                lhsT=stationary[0][:, stationary_cols].bitcast(FP8X4),
-                lhsT_scale=stationary[1][:, stationary_cols],
-                rhs=moving[0][:, moving_cols].bitcast(FP8X4),
-                rhs_scale=moving[1][:, moving_cols],
+                out=bank[:],
+                lhsT=features[0][:, feature_cols].bitcast(FP8X4),
+                lhsT_scale=features[1][:, feature_cols],
+                rhs=psi[0][:].bitcast(FP8X4),
+                rhs_scale=psi[1][:],
                 start=True,
                 stop=True,
             )
+            products.append((s, block, bank))
 
-        def pool_product(s, block, features, feature_cols, psi, absolute):
-            bank = mx_psum.tile([P, BANK], F32, tag="mx")
-            mx_pass(bank[:], features, feature_cols, psi, slice(0, POINTS))
-            nc.scalar.activation(
-                out=absolute, in_=bank[:], func=ABS, accum_out=sums_by_set[:, s, block : block + 1]
-            )
-
-        def first_layer(s):
-            b, w = divmod(s, WEIGHTINGS)
-            x_cols = slice(w * FEATS, (w + 1) * FEATS)
-            rows = work.tile([P, 2 * POINTS], BF16, tag="f_rows", align_bytes=64)
-            f_rows[s] = rows
-            for j in range(WAVELETS):
-                if j < 2:
-                    absolute = rows[:, j * POINTS : (j + 1) * POINTS]
+        def pool_products():
+            for s, block, bank in products:
+                if block in (1, 2):
+                    if block == 1:
+                        rows = work.tile([P, 2 * POINTS], BF16, tag="f_rows", align_bytes=64)
+                        f_rows[s] = rows
+                    absolute = f_rows[s][:, (block - 1) * POINTS : block * POINTS]
                 else:
-                    absolute = unread(s)
-                pool_product(s, 1 + j, x_mx[b], x_cols, psi_mx[s][j], absolute)
+                    scratch = work.tile([P, POINTS], BF16, tag="absolute")
+                    absolute = scratch[:]
+                nc.scalar.activation(
+                    out=absolute, in_=bank[:], func=ABS, accum_out=sums_by_set[:, s, block : block + 1]
+                )
+            products.clear()
 
-        def unread(s):
-            tile = work.tile([P, POINTS], BF16, tag="absolute")
-            return tile[:]
+        def first_layer(unit):
+            s, j = divmod(unit, WAVELETS)
+            multiply(s, 1 + j, x_mx[s], slice(0, FEATS), psi_mx[unit])
+
+        def second_layer(s, i):
+            j, k = SECOND[i]
+            multiply(s, 1 + WAVELETS + i, f_mx[s], slice(j * FEATS, (j + 1) * FEATS), psi_mx[s * WAVELETS + k])
 
         def transpose_f(s):
             pairs = f_rows[s][:].bitcast(F32)
@@ -196,40 +195,57 @@ def tile_simplicialfeatlearninglayertri_pb_t_kernel(tc, x_nodes, p1, p2, p4, p8,
             nc.vector.quantize_mx(out=codes[:].bitcast(FP8X4), scales=scales[:], in_=f_grouped[s][:])
             f_mx[s] = (codes, scales)
 
-        def second_layer(s):
-            block = 1 + WAVELETS
-            for j in range(WAVELETS):
-                for k in range(j + 1, WAVELETS):
-                    pool_product(s, block, f_mx[s], slice(j * FEATS, (j + 1) * FEATS), psi_mx[s][k], unread(s))
-                    block += 1
+        x_grouped = {}
 
-        def load_ahead(s):
-            if s < SETS:
-                if s % WEIGHTINGS == 0:
-                    load_cloud(s // WEIGHTINGS)
-                load_set(s)
+        def due(step, offset):
+            s, rest = divmod(step - offset, WAVELETS)
+            return s if rest == 0 and 0 <= s < SETS else None
 
-        for s in range(LOADS_AHEAD):
-            load_ahead(s)
-        prepare_cloud(0)
-        subtract(0)
-        transpose(0)
-        quantise_psi(0)
-        for s in range(SETS):
-            following = s + 1
-            load_ahead(s + LOADS_AHEAD)
-            if following < SETS:
-                subtract(following)
-            first_layer(s)
-            if following < SETS:
-                transpose(following)
-            transpose_f(s)
-            quantise_f(s)
-            if following < SETS:
-                quantise_psi(following)
-            if s % WEIGHTINGS == WEIGHTINGS - 2 and s + 2 < SETS:
-                prepare_cloud((s + 2) // WEIGHTINGS)
-            second_layer(s)
+        ctx.enter_context(tc.manual_schedule())
+        for s in range(LOAD_BUFS):
+            for j in range(WAVELETS + 1):
+                load_power(s, j)
+                if (s, j) == (0, 1):
+                    load_cloud(0)
+        for step in range(-2, UNITS + 8):
+            s = due(step, 5)
+            if s is not None:
+                quantise_f(s)
+            unit = step + 2
+            if unit < UNITS:
+                subtract(unit)
+                s, j = divmod(unit, WAVELETS)
+                if s + LOAD_BUFS < SETS:
+                    for i in (j,) if j < 2 else (2, 3):
+                        load_power(s + LOAD_BUFS, i)
+                if unit % (WEIGHTINGS * WAVELETS) == WAVELETS and unit // (WEIGHTINGS * WAVELETS) + 1 < CLOUDS:
+                    load_cloud(unit // (WEIGHTINGS * WAVELETS) + 1)
+            if 0 <= step < UNITS:
+                quantise_psi(step)
+            s = due(step, 0)
+            if s is not None:
+                quantise_x(s)
+            s = due(step, -1)
+            if s is not None:
+                prepare_x(s)
+            pool_products()
+            unit = step + 1
+            if 0 <= unit < UNITS:
+                transpose(unit)
+            s = due(step, 4)
+            if s is not None:
+                transpose_f(s)
+            unit = step - 1
+            if 0 <= unit < UNITS:
+                first_layer(unit)
+            for i in range(WAVELETS):
+                s = due(step, 5 + i)
+                if s is not None:
+                    second_layer(s, i)
+            s = due(step, 2)
+            if s is not None and s % WEIGHTINGS == 0:
+                sum_x(s // WEIGHTINGS)
+        pool_products()
 
         bank = mx_psum.tile([P, BANK], F32, tag="mx")
         nc.tensor.transpose(out=bank[:, 0:P], in_=sums[:], identity=identity[:])

@@ -24,6 +24,7 @@ BLOCKS = 7
 BANK = 512
 ROW_TILES_PER_BANK = BANK // (HALVES * P)
 ONES_COLS = 32
+FIRST_PIECES = 2
 LOAD_BUFS = 4
 UNITS = SETS * WAVELETS
 SECOND = ((0, 1), (0, 2), (1, 2))
@@ -50,33 +51,39 @@ def tile_simplicialfeatlearninglayertri_pb_t_kernel(tc, x_nodes, p1, p2, p4, p8,
         nc.vector.memset(sums[:], 0.0)
         sums_by_set = sums[:, 0 : SETS * BLOCKS].rearrange("d (s i) -> d s i", i=BLOCKS)
 
-        x_rows, x_mx, power_rows, psi_rows, psi_grouped, psi_mx = {}, {}, {}, {}, {}, {}
+        x_rows = const.tile([P, SETS * SLOTS * FEATS], BF16)
+
+        x_grouped, x_mx, power_rows, psi_rows, psi_grouped, psi_mx = {}, {}, {}, {}, {}, {}
         f_rows, f_grouped, f_mx, products = {}, {}, {}, []
 
-        def load_cloud(b):
-            rows = work.tile([P, WEIGHTINGS * SLOTS * FEATS], BF16, tag="x_rows")
+        def x_cols(s):
+            return slice(s * SLOTS * FEATS, (s + 1) * SLOTS * FEATS)
+
+        def load_x(s):
+            b, w = divmod(s, WEIGHTINGS)
             nc.sync.dma_start(
-                out=rows[:].rearrange("c (w r) -> c w r", w=WEIGHTINGS),
-                in_=x_nodes[b].rearrange("w (c t) d -> c w (t d)", t=SLOTS),
+                out=x_rows[:, x_cols(s)], in_=x_nodes[b, w].rearrange("(c t) d -> c (t d)", t=SLOTS)
             )
-            x_rows[b] = rows
 
         def load_power(s, j):
             b, w = divmod(s, WEIGHTINGS)
             rows = load.tile([P, SLOTS * POINTS], BF16, tag="power%d" % j)
-            nc.sync.dma_start(
-                out=rows[:], in_=operators[j][b, w].rearrange("(q t) m -> q (t m)", t=SLOTS)
-            )
             power_rows[s, j] = rows
+            return rows[:], operators[j][b, w].rearrange("(q t) m -> q (t m)", t=SLOTS)
+
+        def load_powers(s, which, pieces):
+            views = [load_power(s, j) for j in which]
+            width = SLOTS * POINTS // pieces
+            for i in range(pieces):
+                for rows, source in views:
+                    cols = slice(i * width, (i + 1) * width)
+                    nc.sync.dma_start(out=rows[:, cols], in_=source[:, cols])
 
         def prepare_x(s):
-            b, w = divmod(s, WEIGHTINGS)
             grouped = work.tile([P, FEATS * SLOTS], BF16, tag="x_grouped", align_bytes=64)
             nc.vector.tensor_copy(
                 out=grouped[:].rearrange("c (d t) -> c d t", t=SLOTS),
-                in_=x_rows[b][:, w * SLOTS * FEATS : (w + 1) * SLOTS * FEATS].rearrange(
-                    "c (t d) -> c d t", t=SLOTS
-                ),
+                in_=x_rows[:, x_cols(s)].rearrange("c (t d) -> c d t", t=SLOTS),
             )
             x_grouped[s] = grouped
 
@@ -90,10 +97,10 @@ def tile_simplicialfeatlearninglayertri_pb_t_kernel(tc, x_nodes, p1, p2, p4, p8,
             bank = mx_psum.tile([P, BANK], F32, tag="mx")
             for w in range(WEIGHTINGS):
                 for t in range(SLOTS):
-                    first = (w * SLOTS + t) * FEATS
+                    first = ((b * WEIGHTINGS + w) * SLOTS + t) * FEATS
                     nc.tensor.matmul(
                         out=bank[:, w * ONES_COLS : (w + 1) * ONES_COLS],
-                        lhsT=x_rows[b][:, first : first + FEATS],
+                        lhsT=x_rows[:, first : first + FEATS],
                         rhs=ones[:],
                         start=(t == 0),
                         stop=(t == SLOTS - 1),
@@ -106,7 +113,13 @@ def tile_simplicialfeatlearninglayertri_pb_t_kernel(tc, x_nodes, p1, p2, p4, p8,
         def subtract(unit):
             s, j = divmod(unit, WAVELETS)
             rows = work.tile([P, SLOTS * POINTS], BF16, tag="psi")
-            nc.vector.tensor_sub(out=rows[:], in0=power_rows[s, j][:], in1=power_rows[s, j + 1][:])
+            pieces = FIRST_PIECES if unit == 0 else 1
+            width = SLOTS * POINTS // pieces
+            for i in range(pieces):
+                cols = slice(i * width, (i + 1) * width)
+                nc.vector.tensor_sub(
+                    out=rows[:, cols], in0=power_rows[s, j][:, cols], in1=power_rows[s, j + 1][:, cols]
+                )
             psi_rows[unit] = rows
 
         def transpose(unit):
@@ -122,7 +135,8 @@ def tile_simplicialfeatlearninglayertri_pb_t_kernel(tc, x_nodes, p1, p2, p4, p8,
                         in_=pairs[:, first : first + HALVES * P - i % HALVES : HALVES],
                         identity=identity[:],
                     )
-                copy = nc.vector.tensor_copy if (unit % WAVELETS, h) == (1, 1) else nc.scalar.copy
+                to_vector = unit >= UNITS - 2 or (unit % 2 == 1 and h == 1)
+                copy = nc.vector.tensor_copy if to_vector else nc.scalar.copy
                 copy(
                     out=grouped_pairs[:, h * BANK : (h + 1) * BANK].rearrange(
                         "c (q a u) -> c q a u", a=ROW_TILES_PER_BANK, u=HALVES
@@ -183,7 +197,8 @@ def tile_simplicialfeatlearninglayertri_pb_t_kernel(tc, x_nodes, p1, p2, p4, p8,
                     identity=identity[:],
                 )
             grouped = work.tile([P, 2 * FEATS * SLOTS], BF16, tag="f_grouped", align_bytes=64)
-            nc.scalar.copy(
+            copy = nc.vector.tensor_copy if s == SETS - 1 else nc.scalar.copy
+            copy(
                 out=grouped[:].bitcast(F32).rearrange("c (j d u) -> c j d u", j=2, u=HALVES),
                 in_=bank[:].rearrange("c (j u d) -> c j d u", j=2, u=HALVES),
             )
@@ -195,39 +210,38 @@ def tile_simplicialfeatlearninglayertri_pb_t_kernel(tc, x_nodes, p1, p2, p4, p8,
             nc.vector.quantize_mx(out=codes[:].bitcast(FP8X4), scales=scales[:], in_=f_grouped[s][:])
             f_mx[s] = (codes, scales)
 
-        x_grouped = {}
-
         def due(step, offset):
             s, rest = divmod(step - offset, WAVELETS)
             return s if rest == 0 and 0 <= s < SETS else None
 
         ctx.enter_context(tc.manual_schedule())
-        for s in range(LOAD_BUFS):
-            for j in range(WAVELETS + 1):
-                load_power(s, j)
-                if (s, j) == (0, 1):
-                    load_cloud(0)
+        load_powers(0, (0, 1), FIRST_PIECES)
+        load_powers(0, (2,), 1)
+        load_x(0)
+        load_powers(0, (3,), 1)
+        for s in range(1, LOAD_BUFS):
+            load_powers(s, (0, 1, 2, 3), 1)
+            load_x(s)
         for step in range(-2, UNITS + 8):
             s = due(step, 5)
             if s is not None:
                 quantise_f(s)
+            s = due(step, 0)
+            if s is not None:
+                prepare_x(s)
             unit = step + 2
             if unit < UNITS:
                 subtract(unit)
                 s, j = divmod(unit, WAVELETS)
                 if s + LOAD_BUFS < SETS:
-                    for i in (j,) if j < 2 else (2, 3):
-                        load_power(s + LOAD_BUFS, i)
-                if unit % (WEIGHTINGS * WAVELETS) == WAVELETS and unit // (WEIGHTINGS * WAVELETS) + 1 < CLOUDS:
-                    load_cloud(unit // (WEIGHTINGS * WAVELETS) + 1)
+                    load_powers(s + LOAD_BUFS, (j,) if j < 2 else (2, 3), 1)
+                    if j == 2:
+                        load_x(s + LOAD_BUFS)
             if 0 <= step < UNITS:
                 quantise_psi(step)
             s = due(step, 0)
             if s is not None:
                 quantise_x(s)
-            s = due(step, -1)
-            if s is not None:
-                prepare_x(s)
             pool_products()
             unit = step + 1
             if 0 <= unit < UNITS:
@@ -243,7 +257,7 @@ def tile_simplicialfeatlearninglayertri_pb_t_kernel(tc, x_nodes, p1, p2, p4, p8,
                 if s is not None:
                     second_layer(s, i)
             s = due(step, 2)
-            if s is not None and s % WEIGHTINGS == 0:
+            if s is not None and s % WEIGHTINGS == WEIGHTINGS - 1:
                 sum_x(s // WEIGHTINGS)
         pool_products()
 

@@ -113,12 +113,18 @@ def tile_simplicialfeatlearninglayertri_pb_t_kernel(tc, x_nodes, p1, p2, p4, p8,
         def subtract(unit):
             s, j = divmod(unit, WAVELETS)
             rows = work.tile([P, SLOTS * POINTS], BF16, tag="psi")
+            minuend, subtrahend = (
+                power_rows[s, i][:].rearrange("q (g u e) -> q u g e", u=HALVES, e=2) for i in (j, j + 1)
+            )
+            difference = rows[:].rearrange("q (u g e) -> q u g e", u=HALVES, e=2)
             pieces = FIRST_PIECES if unit == 0 else 1
-            width = SLOTS * POINTS // pieces
+            width = POINTS // pieces
             for i in range(pieces):
-                cols = slice(i * width, (i + 1) * width)
+                groups = slice(i * width, (i + 1) * width)
                 nc.vector.tensor_sub(
-                    out=rows[:, cols], in0=power_rows[s, j][:, cols], in1=power_rows[s, j + 1][:, cols]
+                    out=difference[:, :, groups, :],
+                    in0=minuend[:, :, groups, :],
+                    in1=subtrahend[:, :, groups, :],
                 )
             psi_rows[unit] = rows
 
@@ -129,13 +135,13 @@ def tile_simplicialfeatlearninglayertri_pb_t_kernel(tc, x_nodes, p1, p2, p4, p8,
             for h in range(SLOTS // ROW_TILES_PER_BANK):
                 bank = pair_psum.tile([P, BANK], F32, tag="pairs")
                 for i in range(BANK // P):
-                    first = h * BANK + (i // HALVES) * HALVES * P + i % HALVES
+                    first = (i % HALVES) * POINTS + (h * ROW_TILES_PER_BANK + i // HALVES) * P
                     nc.tensor.transpose(
                         out=bank[:, i * P : (i + 1) * P],
-                        in_=pairs[:, first : first + HALVES * P - i % HALVES : HALVES],
+                        in_=pairs[:, first : first + P],
                         identity=identity[:],
                     )
-                to_vector = unit >= UNITS - 2 or (unit % 2 == 1 and h == 1)
+                to_vector = unit >= UNITS - 2 or (unit % WAVELETS == 1 and h == 1)
                 copy = nc.vector.tensor_copy if to_vector else nc.scalar.copy
                 copy(
                     out=grouped_pairs[:, h * BANK : (h + 1) * BANK].rearrange(
@@ -153,15 +159,16 @@ def tile_simplicialfeatlearninglayertri_pb_t_kernel(tc, x_nodes, p1, p2, p4, p8,
 
         def multiply(s, block, features, feature_cols, psi):
             bank = mx_psum.tile([P, BANK], F32, tag="mx")
-            nc.tensor.matmul_mx(
-                out=bank[:],
-                lhsT=features[0][:, feature_cols].bitcast(FP8X4),
-                lhsT_scale=features[1][:, feature_cols],
-                rhs=psi[0][:].bitcast(FP8X4),
-                rhs_scale=psi[1][:],
-                start=True,
-                stop=True,
-            )
+            for i in range(2 if block <= WAVELETS else 1):
+                nc.tensor.matmul_mx(
+                    out=bank[:],
+                    lhsT=features[0][:, feature_cols].bitcast(FP8X4),
+                    lhsT_scale=features[1][:, feature_cols],
+                    rhs=psi[0][:].bitcast(FP8X4),
+                    rhs_scale=psi[1][:],
+                    start=True,
+                    stop=True,
+                )
             products.append((s, block, bank))
 
         def pool_products():

@@ -105,19 +105,15 @@ def tile_simplicialfeatlearninglayertri_pb_t_kernel(tc, x_nodes, p1, p2, p4, p8,
                         start=(t == 0),
                         stop=(t == SLOTS - 1),
                     )
-            nc.scalar.copy(
-                out=sums_by_set[:, b * WEIGHTINGS : (b + 1) * WEIGHTINGS, 0],
-                in_=bank[:, 0 : WEIGHTINGS * ONES_COLS].rearrange("d (w r) -> d w r", r=ONES_COLS)[:, :, 0],
-            )
+            products.append((b * WEIGHTINGS, 0, bank))
 
-        def subtract(unit):
-            s, j = divmod(unit, WAVELETS)
+        def subtract(s, j):
             rows = work.tile([P, SLOTS * POINTS], BF16, tag="psi")
             minuend, subtrahend = (
                 power_rows[s, i][:].rearrange("q (g u e) -> q u g e", u=HALVES, e=2) for i in (j, j + 1)
             )
             difference = rows[:].rearrange("q (u g e) -> q u g e", u=HALVES, e=2)
-            pieces = FIRST_PIECES if unit == 0 else 1
+            pieces = FIRST_PIECES if (s, j) == (0, 0) else 1
             width = POINTS // pieces
             for i in range(pieces):
                 groups = slice(i * width, (i + 1) * width)
@@ -126,10 +122,10 @@ def tile_simplicialfeatlearninglayertri_pb_t_kernel(tc, x_nodes, p1, p2, p4, p8,
                     in0=minuend[:, :, groups, :],
                     in1=subtrahend[:, :, groups, :],
                 )
-            psi_rows[unit] = rows
+            psi_rows[s, j] = rows
 
-        def transpose(unit):
-            pairs = psi_rows[unit][:].bitcast(F32)
+        def transpose(s, j):
+            pairs = psi_rows[s, j][:].bitcast(F32)
             grouped = work.tile([P, POINTS * SLOTS], BF16, tag="psi_grouped", align_bytes=64)
             grouped_pairs = grouped[:].bitcast(F32)
             for h in range(SLOTS // ROW_TILES_PER_BANK):
@@ -141,7 +137,7 @@ def tile_simplicialfeatlearninglayertri_pb_t_kernel(tc, x_nodes, p1, p2, p4, p8,
                         in_=pairs[:, first : first + P],
                         identity=identity[:],
                     )
-                to_vector = unit >= UNITS - 2 or (unit % WAVELETS == 1 and h == 1)
+                to_vector = (j, h) == (1, 1) or (s >= SETS - 2 and (j, h) == (2, 1))
                 copy = nc.vector.tensor_copy if to_vector else nc.scalar.copy
                 copy(
                     out=grouped_pairs[:, h * BANK : (h + 1) * BANK].rearrange(
@@ -149,30 +145,35 @@ def tile_simplicialfeatlearninglayertri_pb_t_kernel(tc, x_nodes, p1, p2, p4, p8,
                     ),
                     in_=bank[:].rearrange("c (a u q) -> c q a u", a=ROW_TILES_PER_BANK, u=HALVES),
                 )
-            psi_grouped[unit] = grouped
+            psi_grouped[s, j] = grouped
 
-        def quantise_psi(unit):
-            codes = work.tile([P, POINTS], U32, tag="psi_codes%d" % (unit % WAVELETS), align_bytes=64)
-            scales = work.tile([P, POINTS], U8, tag="psi_scales%d" % (unit % WAVELETS), align_bytes=64)
-            nc.vector.quantize_mx(out=codes[:].bitcast(FP8X4), scales=scales[:], in_=psi_grouped[unit][:])
-            psi_mx[unit] = (codes, scales)
+        def quantise_psi(s, j):
+            codes = work.tile([P, POINTS], U32, tag="psi_codes%d" % j, align_bytes=64)
+            scales = work.tile([P, POINTS], U8, tag="psi_scales%d" % j, align_bytes=64)
+            nc.vector.quantize_mx(out=codes[:].bitcast(FP8X4), scales=scales[:], in_=psi_grouped[s, j][:])
+            psi_mx[s, j] = (codes, scales)
 
         def multiply(s, block, features, feature_cols, psi):
             bank = mx_psum.tile([P, BANK], F32, tag="mx")
-            for i in range(2 if block <= WAVELETS else 1):
-                nc.tensor.matmul_mx(
-                    out=bank[:],
-                    lhsT=features[0][:, feature_cols].bitcast(FP8X4),
-                    lhsT_scale=features[1][:, feature_cols],
-                    rhs=psi[0][:].bitcast(FP8X4),
-                    rhs_scale=psi[1][:],
-                    start=True,
-                    stop=True,
-                )
+            nc.tensor.matmul_mx(
+                out=bank[:],
+                lhsT=features[0][:, feature_cols].bitcast(FP8X4),
+                lhsT_scale=features[1][:, feature_cols],
+                rhs=psi[0][:].bitcast(FP8X4),
+                rhs_scale=psi[1][:],
+                start=True,
+                stop=True,
+            )
             products.append((s, block, bank))
 
         def pool_products():
             for s, block, bank in products:
+                if block == 0:
+                    nc.scalar.copy(
+                        out=sums_by_set[:, s : s + WEIGHTINGS, 0],
+                        in_=bank[:, 0 : WEIGHTINGS * ONES_COLS].rearrange("d (w r) -> d w r", r=ONES_COLS)[:, :, 0],
+                    )
+                    continue
                 if block in (1, 2):
                     if block == 1:
                         rows = work.tile([P, 2 * POINTS], BF16, tag="f_rows", align_bytes=64)
@@ -186,13 +187,12 @@ def tile_simplicialfeatlearninglayertri_pb_t_kernel(tc, x_nodes, p1, p2, p4, p8,
                 )
             products.clear()
 
-        def first_layer(unit):
-            s, j = divmod(unit, WAVELETS)
-            multiply(s, 1 + j, x_mx[s], slice(0, FEATS), psi_mx[unit])
+        def first_layer(s, j):
+            multiply(s, 1 + j, x_mx[s], slice(0, FEATS), psi_mx[s, j])
 
         def second_layer(s, i):
             j, k = SECOND[i]
-            multiply(s, 1 + WAVELETS + i, f_mx[s], slice(j * FEATS, (j + 1) * FEATS), psi_mx[s * WAVELETS + k])
+            multiply(s, 1 + WAVELETS + i, f_mx[s], slice(j * FEATS, (j + 1) * FEATS), psi_mx[s, k])
 
         def transpose_f(s):
             pairs = f_rows[s][:].bitcast(F32)
@@ -217,9 +217,16 @@ def tile_simplicialfeatlearninglayertri_pb_t_kernel(tc, x_nodes, p1, p2, p4, p8,
             nc.vector.quantize_mx(out=codes[:].bitcast(FP8X4), scales=scales[:], in_=f_grouped[s][:])
             f_mx[s] = (codes, scales)
 
-        def due(step, offset):
-            s, rest = divmod(step - offset, WAVELETS)
-            return s if rest == 0 and 0 <= s < SETS else None
+        order = [(s, j) for s in range(SETS - 2) for j in range(WAVELETS)]
+        order += [(s, j) for s in (SETS - 2, SETS - 1) for j in (0, 1)]
+        order += [(s, 2) for s in (SETS - 2, SETS - 1)]
+
+        def at(position):
+            return order[position] if 0 <= position < UNITS else (0, -1)
+
+        def sets_whose(j, position):
+            s, i = at(position)
+            return [s] if i == j else []
 
         ctx.enter_context(tc.manual_schedule())
         load_powers(0, (0, 1), FIRST_PIECES)
@@ -230,42 +237,37 @@ def tile_simplicialfeatlearninglayertri_pb_t_kernel(tc, x_nodes, p1, p2, p4, p8,
             load_powers(s, (0, 1, 2, 3), 1)
             load_x(s)
         for step in range(-2, UNITS + 8):
-            s = due(step, 5)
-            if s is not None:
-                quantise_f(s)
-            s = due(step, 0)
-            if s is not None:
+            for s in sets_whose(0, step):
                 prepare_x(s)
-            unit = step + 2
-            if unit < UNITS:
-                subtract(unit)
-                s, j = divmod(unit, WAVELETS)
+            for s in sets_whose(1, step - 4):
+                quantise_f(s)
+            s, j = at(step + 2)
+            if j >= 0:
+                subtract(s, j)
                 if s + LOAD_BUFS < SETS:
                     load_powers(s + LOAD_BUFS, (j,) if j < 2 else (2, 3), 1)
                     if j == 2:
                         load_x(s + LOAD_BUFS)
-            if 0 <= step < UNITS:
-                quantise_psi(step)
-            s = due(step, 0)
-            if s is not None:
+            s, j = at(step)
+            if j >= 0:
+                quantise_psi(s, j)
+            for s in sets_whose(0, step):
                 quantise_x(s)
             pool_products()
-            unit = step + 1
-            if 0 <= unit < UNITS:
-                transpose(unit)
-            s = due(step, 4)
-            if s is not None:
+            s, j = at(step + 1)
+            if j >= 0:
+                transpose(s, j)
+            for s in sets_whose(1, step - 2):
                 transpose_f(s)
-            unit = step - 1
-            if 0 <= unit < UNITS:
-                first_layer(unit)
+            s, j = at(step - 1)
+            if j >= 0:
+                first_layer(s, j)
             for i in range(WAVELETS):
-                s = due(step, 5 + i)
-                if s is not None:
+                for s in sets_whose(1, step - 4 - i):
                     second_layer(s, i)
-            s = due(step, 2)
-            if s is not None and s % WEIGHTINGS == WEIGHTINGS - 1:
-                sum_x(s // WEIGHTINGS)
+            for s in sets_whose(0, step - 2):
+                if s % WEIGHTINGS == 2:
+                    sum_x(s // WEIGHTINGS)
         pool_products()
 
         bank = mx_psum.tile([P, BANK], F32, tag="mx")

@@ -109,18 +109,12 @@ def tile_simplicialfeatlearninglayertri_pb_t_kernel(tc, x_nodes, p1, p2, p4, p8,
 
         def subtract(s, j):
             rows = work.tile([P, SLOTS * POINTS], BF16, tag="psi")
-            minuend, subtrahend = (
-                power_rows[s, i][:].rearrange("q (g u e) -> q u g e", u=HALVES, e=2) for i in (j, j + 1)
-            )
-            difference = rows[:].rearrange("q (u g e) -> q u g e", u=HALVES, e=2)
             pieces = FIRST_PIECES if (s, j) == (0, 0) else 1
-            width = POINTS // pieces
+            width = SLOTS * POINTS // pieces
             for i in range(pieces):
-                groups = slice(i * width, (i + 1) * width)
+                cols = slice(i * width, (i + 1) * width)
                 nc.vector.tensor_sub(
-                    out=difference[:, :, groups, :],
-                    in0=minuend[:, :, groups, :],
-                    in1=subtrahend[:, :, groups, :],
+                    out=rows[:, cols], in0=power_rows[s, j][:, cols], in1=power_rows[s, j + 1][:, cols]
                 )
             psi_rows[s, j] = rows
 
@@ -131,10 +125,10 @@ def tile_simplicialfeatlearninglayertri_pb_t_kernel(tc, x_nodes, p1, p2, p4, p8,
             for h in range(SLOTS // ROW_TILES_PER_BANK):
                 bank = pair_psum.tile([P, BANK], F32, tag="pairs")
                 for i in range(BANK // P):
-                    first = (i % HALVES) * POINTS + (h * ROW_TILES_PER_BANK + i // HALVES) * P
+                    first = h * BANK + (i // HALVES) * HALVES * P + i % HALVES
                     nc.tensor.transpose(
                         out=bank[:, i * P : (i + 1) * P],
-                        in_=pairs[:, first : first + P],
+                        in_=pairs[:, first : first + HALVES * P - i % HALVES : HALVES],
                         identity=identity[:],
                     )
                 to_vector = (j, h) == (1, 1) or (s >= SETS - 2 and (j, h) == (2, 1))

@@ -27,6 +27,8 @@ ONES_COLS = 32
 FIRST_PIECES = 2
 LOAD_BUFS = 4
 UNITS = SETS * WAVELETS
+LATE_ON_VECTOR = ((SETS - 2, 6), (SETS - 1, 3))
+RUN = 4
 SECOND = ((0, 1), (0, 2), (1, 2))
 
 FLOPS = 2 * POINTS * POINTS * FEATS * 6 * SETS
@@ -82,8 +84,8 @@ def tile_simplicialfeatlearninglayertri_pb_t_kernel(tc, x_nodes, p1, p2, p4, p8,
         def prepare_x(s):
             grouped = work.tile([P, FEATS * SLOTS], BF16, tag="x_grouped", align_bytes=64)
             nc.vector.tensor_copy(
-                out=grouped[:].rearrange("c (d t) -> c d t", t=SLOTS),
-                in_=x_rows[:, x_cols(s)].rearrange("c (t d) -> c d t", t=SLOTS),
+                out=grouped[:].rearrange("c (d i t) -> c d t i", i=RUN, t=SLOTS),
+                in_=x_rows[:, x_cols(s)].rearrange("c (t d i) -> c d t i", i=RUN, t=SLOTS),
             )
             x_grouped[s] = grouped
 
@@ -131,7 +133,7 @@ def tile_simplicialfeatlearninglayertri_pb_t_kernel(tc, x_nodes, p1, p2, p4, p8,
                         in_=pairs[:, first : first + HALVES * P - i % HALVES : HALVES],
                         identity=identity[:],
                     )
-                to_vector = (j, h) == (1, 1) or (s >= SETS - 2 and (j, h) == (2, 1))
+                to_vector = (s >= 2 and (j, h) == (2, 1)) or (s >= SETS - 2 and (j, h) == (0, 1))
                 copy = nc.vector.tensor_copy if to_vector else nc.scalar.copy
                 copy(
                     out=grouped_pairs[:, h * BANK : (h + 1) * BANK].rearrange(
@@ -173,6 +175,17 @@ def tile_simplicialfeatlearninglayertri_pb_t_kernel(tc, x_nodes, p1, p2, p4, p8,
                         rows = work.tile([P, 2 * POINTS], BF16, tag="f_rows", align_bytes=64)
                         f_rows[s] = rows
                     absolute = f_rows[s][:, (block - 1) * POINTS : block * POINTS]
+                elif (s, block) in LATE_ON_VECTOR:
+                    values = work.tile([P, POINTS], F32, tag="values")
+                    nc.vector.tensor_copy(out=values[:], in_=bank[:])
+                    nc.vector.tensor_reduce(
+                        out=sums_by_set[:, s, block : block + 1],
+                        in_=values[:],
+                        axis=mybir.AxisListType.X,
+                        op=mybir.AluOpType.add,
+                        apply_absolute_value=True,
+                    )
+                    continue
                 else:
                     scratch = work.tile([P, POINTS], BF16, tag="absolute")
                     absolute = scratch[:]

from contextlib import ExitStack

import concourse.mybir as mybir
from concourse.masks import make_identity

F32 = mybir.dt.float32
BF16 = mybir.dt.bfloat16
U32 = mybir.dt.uint32
U8 = mybir.dt.uint8
FP8X4 = mybir.dt.float8_e4m3fn_x4
ABS = mybir.ActivationFunctionType.Abs
COPY = mybir.ActivationFunctionType.Copy

CLOUDS = 4
WEIGHTINGS = 4
SETS = CLOUDS * WEIGHTINGS
POINTS = 512
FEATS = 128
P = 128
SLOTS = 4
HALVES = 2
WAVELETS = 3
BLOCKS = 7
BANK = 512
ROW_TILES_PER_BANK = BANK // (HALVES * P)
ONES_COLS = 32
FIRST_PIECES = 2
LOAD_BUFS = 4
UNITS = SETS * WAVELETS
LATE_ON_VECTOR = ((SETS - 2, 6), (SETS - 1, 3))
RUN = 4
SECOND = ((0, 1), (0, 2), (1, 2))

FLOPS = 2 * POINTS * POINTS * FEATS * 6 * SETS


def tile_simplicialfeatlearninglayertri_pb_t_kernel(tc, x_nodes, p1, p2, p4, p8, out):
    nc = tc.nc
    operators = (p1, p2, p4, p8)

    with ExitStack() as ctx:
        const = ctx.enter_context(tc.tile_pool(name="const", bufs=1))
        load = ctx.enter_context(tc.tile_pool(name="load", bufs=LOAD_BUFS))
        work = ctx.enter_context(tc.tile_pool(name="work", bufs=3))
        pair_psum = ctx.enter_context(tc.psum_pool(name="pair_psum", bufs=4))
        mx_psum = ctx.enter_context(tc.psum_pool(name="mx_psum", bufs=4))

        identity = const.tile([P, P], F32)
        make_identity(nc, identity[:])
        ones = const.tile([P, ONES_COLS], BF16)
        nc.vector.memset(ones[:], 1.0)
        sums = const.tile([P, P], F32)
        nc.vector.memset(sums[:], 0.0)
        sums_by_set = sums[:, 0 : SETS * BLOCKS].rearrange("d (s i) -> d s i", i=BLOCKS)

        x_rows = const.tile([P, SETS * SLOTS * FEATS], BF16)

        x_grouped, x_mx, power_rows, psi_rows, psi_grouped, psi_mx = {}, {}, {}, {}, {}, {}
        f_rows, f_grouped, f_mx, products = {}, {}, {}, []

        def x_cols(s):
            return slice(s * SLOTS * FEATS, (s + 1) * SLOTS * FEATS)

        def load_x(s):
            b, w = divmod(s, WEIGHTINGS)
            nc.sync.dma_start(
                out=x_rows[:, x_cols(s)], in_=x_nodes[b, w].rearrange("(c t) d -> c (t d)", t=SLOTS)
            )

        def load_power(s, j):
            b, w = divmod(s, WEIGHTINGS)
            rows = load.tile([P, SLOTS * POINTS], BF16, tag="power%d" % j)
            power_rows[s, j] = rows
            return rows[:], operators[j][b, w].rearrange("(q t) m -> q (t m)", t=SLOTS)

        def load_powers(s, which, pieces):
            views = [load_power(s, j) for j in which]
            width = SLOTS * POINTS // pieces
            for i in range(pieces):
                for rows, source in views:
                    cols = slice(i * width, (i + 1) * width)
                    nc.sync.dma_start(out=rows[:, cols], in_=source[:, cols])

        def prepare_x(s):
            grouped = work.tile([P, FEATS * SLOTS], BF16, tag="x_grouped", align_bytes=64)
            nc.vector.tensor_copy(
                out=grouped[:].rearrange("c (d i t) -> c d t i", i=RUN, t=SLOTS),
                in_=x_rows[:, x_cols(s)].rearrange("c (t d i) -> c d t i", i=RUN, t=SLOTS),
            )
            x_grouped[s] = grouped

        def quantise_x(s):
            codes = work.tile([P, FEATS], U32, tag="x_codes", align_bytes=64)
            scales = work.tile([P, FEATS], U8, tag="x_scales", align_bytes=64)
            nc.vector.quantize_mx(out=codes[:].bitcast(FP8X4), scales=scales[:], in_=x_grouped[s][:])
            x_mx[s] = (codes, scales)

        def sum_x(b):
            bank = mx_psum.tile([P, BANK], F32, tag="mx")
            for w in range(WEIGHTINGS):
                for t in range(SLOTS):
                    first = ((b * WEIGHTINGS + w) * SLOTS + t) * FEATS
                    nc.tensor.matmul(
                        out=bank[:, w * ONES_COLS : (w + 1) * ONES_COLS],
                        lhsT=x_rows[:, first : first + FEATS],
                        rhs=ones[:],
                        start=(t == 0),
                        stop=(t == SLOTS - 1),
                    )
            products.append((b * WEIGHTINGS, 0, bank))

        def subtract(s, j):
            rows = work.tile([P, SLOTS * POINTS], BF16, tag="psi")
            pieces = FIRST_PIECES if (s, j) == (0, 0) else 1
            width = SLOTS * POINTS // pieces
            for i in range(pieces):
                cols = slice(i * width, (i + 1) * width)
                nc.vector.tensor_sub(
                    out=rows[:, cols], in0=power_rows[s, j][:, cols], in1=power_rows[s, j + 1][:, cols]
                )
            psi_rows[s, j] = rows

        def transpose(s, j):
            pairs = psi_rows[s, j][:].bitcast(F32)
            grouped = work.tile([P, POINTS * SLOTS], BF16, tag="psi_grouped", align_bytes=64)
            grouped_pairs = grouped[:].bitcast(F32)
            for h in range(SLOTS // ROW_TILES_PER_BANK):
                bank = pair_psum.tile([P, BANK], F32, tag="pairs")
                for i in range(BANK // P):
                    first = h * BANK + (i // HALVES) * HALVES * P + i % HALVES
                    nc.tensor.transpose(
                        out=bank[:, i * P : (i + 1) * P],
                        in_=pairs[:, first : first + HALVES * P - i % HALVES : HALVES],
                        identity=identity[:],
                    )
                to_vector = (s >= 2 and (j, h) == (2, 1)) or (s >= SETS - 2 and (j, h) == (0, 1))
                copy = nc.vector.tensor_copy if to_vector else nc.scalar.copy
                copy(
                    out=grouped_pairs[:, h * BANK : (h + 1) * BANK].rearrange(
                        "c (q a u) -> c q a u", a=ROW_TILES_PER_BANK, u=HALVES
                    ),
                    in_=bank[:].rearrange("c (a u q) -> c q a u", a=ROW_TILES_PER_BANK, u=HALVES),
                )
            psi_grouped[s, j] = grouped

        def quantise_psi(s, j):
            codes = work.tile([P, POINTS], U32, tag="psi_codes%d" % j, align_bytes=64)
            scales = work.tile([P, POINTS], U8, tag="psi_scales%d" % j, align_bytes=64)
            nc.vector.quantize_mx(out=codes[:].bitcast(FP8X4), scales=scales[:], in_=psi_grouped[s, j][:])
            psi_mx[s, j] = (codes, scales)

        def multiply(s, block, features, feature_cols, psi):
            bank = mx_psum.tile([P, BANK], F32, tag="mx")
            nc.tensor.matmul_mx(
                out=bank[:],
                lhsT=features[0][:, feature_cols].bitcast(FP8X4),
                lhsT_scale=features[1][:, feature_cols],
                rhs=psi[0][:].bitcast(FP8X4),
                rhs_scale=psi[1][:],
                start=True,
                stop=True,
            )
            products.append((s, block, bank))

        def pool_products():
            for s, block, bank in products:
                if block == 0:
                    nc.scalar.copy(
                        out=sums_by_set[:, s : s + WEIGHTINGS, 0],
                        in_=bank[:, 0 : WEIGHTINGS * ONES_COLS].rearrange("d (w r) -> d w r", r=ONES_COLS)[:, :, 0],
                    )
                    continue
                if block in (1, 2):
                    if block == 1:
                        rows = work.tile([P, 2 * POINTS], BF16, tag="f_rows", align_bytes=64)
                        f_rows[s] = rows
                    absolute = f_rows[s][:, (block - 1) * POINTS : block * POINTS]
                elif (s, block) in LATE_ON_VECTOR:
                    values = work.tile([P, POINTS], F32, tag="values")
                    nc.vector.tensor_copy(out=values[:], in_=bank[:])
                    nc.vector.tensor_reduce(
                        out=sums_by_set[:, s, block : block + 1],
                        in_=values[:],
                        axis=mybir.AxisListType.X,
                        op=mybir.AluOpType.add,
                        apply_absolute_value=True,
                    )
                    continue
                else:
                    scratch = work.tile([P, POINTS], BF16, tag="absolute")
                    absolute = scratch[:]
                nc.scalar.activation(
                    out=absolute, in_=bank[:], func=ABS, accum_out=sums_by_set[:, s, block : block + 1]
                )
            products.clear()

        def first_layer(s, j):
            multiply(s, 1 + j, x_mx[s], slice(0, FEATS), psi_mx[s, j])

        def second_layer(s, i):
            j, k = SECOND[i]
            multiply(s, 1 + WAVELETS + i, f_mx[s], slice(j * FEATS, (j + 1) * FEATS), psi_mx[s, k])

        def transpose_f(s):
            pairs = f_rows[s][:].bitcast(F32)
            bank = pair_psum.tile([P, BANK], F32, tag="pairs")
            for i in range(BANK // P):
                nc.tensor.transpose(
                    out=bank[:, i * P : (i + 1) * P],
                    in_=pairs[:, i * P : (i + 1) * P],
                    identity=identity[:],
                )
            grouped = work.tile([P, 2 * FEATS * SLOTS], BF16, tag="f_grouped", align_bytes=64)
            copy = nc.vector.tensor_copy if s == SETS - 1 else nc.scalar.copy
            copy(
                out=grouped[:].bitcast(F32).rearrange("c (j d u) -> c j d u", j=2, u=HALVES),
                in_=bank[:].rearrange("c (j u d) -> c j d u", j=2, u=HALVES),
            )
            f_grouped[s] = grouped

        def quantise_f(s):
            codes = work.tile([P, 2 * FEATS], U32, tag="f_codes", align_bytes=64)
            scales = work.tile([P, 2 * FEATS], U8, tag="f_scales", align_bytes=64)
            nc.vector.quantize_mx(out=codes[:].bitcast(FP8X4), scales=scales[:], in_=f_grouped[s][:])
            f_mx[s] = (codes, scales)

        order = [(s, j) for s in range(SETS - 2) for j in range(WAVELETS)]
        order += [(s, j) for s in (SETS - 2, SETS - 1) for j in (0, 1)]
        order += [(s, 2) for s in (SETS - 2, SETS - 1)]

        def at(position):
            return order[position] if 0 <= position < UNITS else (0, -1)

        def sets_whose(j, position):
            s, i = at(position)
            return [s] if i == j else []

        ctx.enter_context(tc.manual_schedule())
        load_powers(0, (0, 1), FIRST_PIECES)
        load_powers(0, (2,), 1)
        load_x(0)
        load_powers(0, (3,), 1)
        for s in range(1, LOAD_BUFS):
            load_powers(s, (0, 1, 2, 3), 1)
            load_x(s)
        for step in range(-2, UNITS + 8):
            for s in sets_whose(0, step):
                prepare_x(s)
            for s in sets_whose(1, step - 4):
                quantise_f(s)
            s, j = at(step + 2)
            if j >= 0:
                subtract(s, j)
                if s + LOAD_BUFS < SETS:
                    load_powers(s + LOAD_BUFS, (j,) if j < 2 else (2, 3), 1)
                    if j == 2:
                        load_x(s + LOAD_BUFS)
            s, j = at(step)
            if j >= 0:
                quantise_psi(s, j)
            for s in sets_whose(0, step):
                quantise_x(s)
            pool_products()
            s, j = at(step + 1)
            if j >= 0:
                transpose(s, j)
            for s in sets_whose(1, step - 2):
                transpose_f(s)
            s, j = at(step - 1)
            if j >= 0:
                first_layer(s, j)
            for i in range(WAVELETS):
                for s in sets_whose(1, step - 4 - i):
                    second_layer(s, i)
            for s in sets_whose(0, step - 2):
                if s % WEIGHTINGS == 2:
                    sum_x(s // WEIGHTINGS)
        pool_products()

        bank = mx_psum.tile([P, BANK], F32, tag="mx")
        nc.tensor.transpose(out=bank[:, 0:P], in_=sums[:], identity=identity[:])
        means = const.tile([P, FEATS], F32)
        nc.scalar.activation(out=means[:], in_=bank[:, 0:P], func=COPY, scale=1.0 / POINTS)
        nc.sync.dma_start(
            out=out.rearrange("b (r d) -> (b r) d", d=FEATS), in_=means[0 : SETS * BLOCKS, :]
        )
